import numpy as np
import ml_dtypes

BF16 = ml_dtypes.bfloat16


def bf(x):
    return np.asarray(x, np.float32).astype(BF16)


def f32(x):
    return np.asarray(x, np.float32)


def f64(x):
    return np.asarray(x).astype(np.float64)


def striped(idx):
    return np.tile(idx.reshape(-1, 16).T, (8, 1))


C, S, T, K, N, COLS = 1024, 256, 256, 8, 2048, 16


def setup_inputs():
    return {"x": f32(np.random.standard_normal((C, S))), "offs": striped(np.concatenate([np.random.permutation(S) for _ in range(-(-(N) // S))])[:N])}


def reference(x, offs):
    idx = offs[:16].T.reshape(-1)
    votes = np.maximum(f64(x), 0.0)[:, idx].reshape(C, K, T)
    return votes.sum(axis=1) / COLS

@@ -1,0 +1,47 @@
+import concourse.mybir as mybir
+
+F32 = mybir.dt.float32
+U16 = mybir.dt.uint16
+ADD = mybir.AluOpType.add
+RELU = mybir.ActivationFunctionType.Relu
+
+P = 128
+PLANES = 1024
+PIXELS = 256
+BINS = 256
+VOTERS = 8
+WIDTH = 16
+BLOCKS = PLANES // P
+PIECE = BINS // 16
+
+
+def tile_ht_kernel(tc, x, offs, out):
+    nc = tc.nc
+    x_blocks = x.rearrange("(b p) s -> b p s", p=P)
+    out_blocks = out.rearrange("(b p) t -> b p t", p=P)
+
+    with (
+        tc.tile_pool(name="held", bufs=1) as held,
+        tc.tile_pool(name="blocks", bufs=BLOCKS) as blocks,
+    ):
+        offsets = held.tile([P, VOTERS * PIECE], U16, name="offsets")
+        nc.sync.dma_start(offsets[:], offs)
+
+        zeros = held.tile([P, BINS], F32, name="zeros")
+        nc.vector.memset(zeros[:], 0.0)
+
+        for b in range(BLOCKS):
+            pixels = blocks.tile([P, PIXELS], F32, name="pixels")
+            nc.sync.dma_start(pixels[:], x_blocks[b])
+
+            votes = blocks.tile([P, PIXELS], F32, name="votes")
+            nc.scalar.activation(votes[:], pixels[:], RELU, scale=1.0 / WIDTH)
+
+            sums = zeros
+            for k in range(VOTERS):
+                earlier = sums
+                sums = blocks.tile([P, BINS], F32, name="sums")
+                picked = votes[:].indirect(offsets[:, k * PIECE : (k + 1) * PIECE])
+                nc.vector.tensor_tensor(sums[:], picked, earlier[:], ADD)
+
+            nc.sync.dma_start(out_blocks[b], sums[:])

@@ -13,6 +13,7 @@ VOTERS = 8
 WIDTH = 16
 BLOCKS = PLANES // P
 PIECE = BINS // 16
+LANES = 2
 
 
 def tile_ht_kernel(tc, x, offs, out):
@@ -23,6 +24,7 @@ def tile_ht_kernel(tc, x, offs, out):
     with (
         tc.tile_pool(name="held", bufs=1) as held,
         tc.tile_pool(name="blocks", bufs=BLOCKS) as blocks,
+        tc.tile_pool(name="ring", bufs=LANES * VOTERS) as ring,
     ):
         offsets = held.tile([P, VOTERS * PIECE], U16, name="offsets")
         nc.sync.dma_start(offsets[:], offs)
@@ -30,18 +32,21 @@ def tile_ht_kernel(tc, x, offs, out):
         zeros = held.tile([P, BINS], F32, name="zeros")
         nc.vector.memset(zeros[:], 0.0)
 
-        for b in range(BLOCKS):
-            pixels = blocks.tile([P, PIXELS], F32, name="pixels")
-            nc.sync.dma_start(pixels[:], x_blocks[b])
+        for first in range(0, BLOCKS, LANES):
+            votes = []
+            for lane in range(LANES):
+                pixels = blocks.tile([P, PIXELS], F32, name="pixels")
+                nc.sync.dma_start(pixels[:], x_blocks[first + lane])
+                votes.append(blocks.tile([P, PIXELS], F32, name="votes"))
+                nc.scalar.activation(votes[lane][:], pixels[:], RELU, scale=1.0 / WIDTH)
 
-            votes = blocks.tile([P, PIXELS], F32, name="votes")
-            nc.scalar.activation(votes[:], pixels[:], RELU, scale=1.0 / WIDTH)
-
-            sums = zeros
+            sums = [zeros] * LANES
             for k in range(VOTERS):
-                earlier = sums
-                sums = blocks.tile([P, BINS], F32, name="sums")
-                picked = votes[:].indirect(offsets[:, k * PIECE : (k + 1) * PIECE])
-                nc.vector.tensor_tensor(sums[:], picked, earlier[:], ADD)
+                for lane in range(LANES):
+                    earlier = sums[lane]
+                    sums[lane] = ring.tile([P, BINS], F32, name="sums")
+                    picked = votes[lane][:].indirect(offsets[:, k * PIECE : (k + 1) * PIECE])
+                    nc.vector.tensor_tensor(sums[lane][:], picked, earlier[:], ADD)
 
-            nc.sync.dma_start(out_blocks[b], sums[:])
+            for lane in range(LANES):
+                nc.sync.dma_start(out_blocks[first + lane], sums[lane][:])

@@ -3,6 +3,8 @@ import concourse.mybir as mybir
 F32 = mybir.dt.float32
 U16 = mybir.dt.uint16
 ADD = mybir.AluOpType.add
+MAX = mybir.AluOpType.max
+MULT = mybir.AluOpType.mult
 RELU = mybir.ActivationFunctionType.Relu
 
 P = 128
@@ -27,7 +29,6 @@ def tile_ht_kernel(tc, x, offs, out):
         tc.tile_pool(name="ring", bufs=LANES * VOTERS) as ring,
     ):
         offsets = held.tile([P, VOTERS * PIECE], U16, name="offsets")
-        nc.sync.dma_start(offsets[:], offs)
 
         zeros = held.tile([P, BINS], F32, name="zeros")
         nc.vector.memset(zeros[:], 0.0)
@@ -37,8 +38,13 @@ def tile_ht_kernel(tc, x, offs, out):
             for lane in range(LANES):
                 pixels = blocks.tile([P, PIXELS], F32, name="pixels")
                 nc.sync.dma_start(pixels[:], x_blocks[first + lane])
+                if first + lane == 0:
+                    nc.sync.dma_start(offsets[:], offs)
                 votes.append(blocks.tile([P, PIXELS], F32, name="votes"))
-                nc.scalar.activation(votes[lane][:], pixels[:], RELU, scale=1.0 / WIDTH)
+                if first + lane == 0:
+                    nc.vector.tensor_scalar(votes[lane][:], pixels[:], 0.0, 1.0 / WIDTH, MAX, MULT)
+                else:
+                    nc.scalar.activation(votes[lane][:], pixels[:], RELU, scale=1.0 / WIDTH)
 
             sums = [zeros] * LANES
             for k in range(VOTERS):

@@ -55,4 +55,4 @@ def tile_ht_kernel(tc, x, offs, out):
                     nc.vector.tensor_tensor(sums[lane][:], picked, earlier[:], ADD)
 
             for lane in range(LANES):
-                nc.sync.dma_start(out_blocks[first + lane], sums[lane][:])
+                nc.scalar.dma_start(out_blocks[first + lane], sums[lane][:])

@@ -3,8 +3,6 @@ import concourse.mybir as mybir
 F32 = mybir.dt.float32
 U16 = mybir.dt.uint16
 ADD = mybir.AluOpType.add
-MAX = mybir.AluOpType.max
-MULT = mybir.AluOpType.mult
 RELU = mybir.ActivationFunctionType.Relu
 
 P = 128
@@ -15,7 +13,7 @@ VOTERS = 8
 WIDTH = 16
 BLOCKS = PLANES // P
 PIECE = BINS // 16
-LANES = 2
+LANES = 4
 
 
 def tile_ht_kernel(tc, x, offs, out):
@@ -33,21 +31,26 @@ def tile_ht_kernel(tc, x, offs, out):
         zeros = held.tile([P, BINS], F32, name="zeros")
         nc.vector.memset(zeros[:], 0.0)
 
+        nc.sync.dma_start(offsets[:], offs)
+
         for first in range(0, BLOCKS, LANES):
+            pixels = []
             votes = []
             for lane in range(LANES):
-                pixels = blocks.tile([P, PIXELS], F32, name="pixels")
-                nc.sync.dma_start(pixels[:], x_blocks[first + lane])
-                if first + lane == 0:
-                    nc.sync.dma_start(offsets[:], offs)
+                pixels.append(blocks.tile([P, PIXELS], F32, name="pixels"))
+                nc.sync.dma_start(pixels[lane][:], x_blocks[first + lane])
                 votes.append(blocks.tile([P, PIXELS], F32, name="votes"))
-                if first + lane == 0:
-                    nc.vector.tensor_scalar(votes[lane][:], pixels[:], 0.0, 1.0 / WIDTH, MAX, MULT)
-                else:
-                    nc.scalar.activation(votes[lane][:], pixels[:], RELU, scale=1.0 / WIDTH)
+                nc.scalar.activation(votes[lane][:], pixels[lane][:], RELU, scale=1.0 / WIDTH)
 
-            sums = [zeros] * LANES
-            for k in range(VOTERS):
+            sums = []
+            for lane in range(LANES):
+                unrectified = ring.tile([P, BINS], F32, name="unrectified")
+                picked = pixels[lane][:].indirect(offsets[:, 0:PIECE])
+                nc.vector.tensor_tensor(unrectified[:], picked, zeros[:], ADD)
+                sums.append(ring.tile([P, BINS], F32, name="sums"))
+                nc.scalar.activation(sums[lane][:], unrectified[:], RELU, scale=1.0 / WIDTH)
+
+            for k in range(1, VOTERS):
                 for lane in range(LANES):
                     earlier = sums[lane]
                     sums[lane] = ring.tile([P, BINS], F32, name="sums")

@@ -13,7 +13,7 @@ VOTERS = 8
 WIDTH = 16
 BLOCKS = PLANES // P
 PIECE = BINS // 16
-LANES = 4
+LANES = 8
 
 
 def tile_ht_kernel(tc, x, offs, out):

@@ -31,14 +31,14 @@ def tile_ht_kernel(tc, x, offs, out):
         zeros = held.tile([P, BINS], F32, name="zeros")
         nc.vector.memset(zeros[:], 0.0)
 
-        nc.sync.dma_start(offsets[:], offs)
-
         for first in range(0, BLOCKS, LANES):
             pixels = []
             votes = []
             for lane in range(LANES):
                 pixels.append(blocks.tile([P, PIXELS], F32, name="pixels"))
                 nc.sync.dma_start(pixels[lane][:], x_blocks[first + lane])
+                if first + lane == 0:
+                    nc.sync.dma_start(offsets[:], offs)
                 votes.append(blocks.tile([P, PIXELS], F32, name="votes"))
                 nc.scalar.activation(votes[lane][:], pixels[lane][:], RELU, scale=1.0 / WIDTH)
 

@@ -13,13 +13,14 @@ VOTERS = 8
 WIDTH = 16
 BLOCKS = PLANES // P
 PIECE = BINS // 16
+PAIR = 2
 LANES = 8
 
 
 def tile_ht_kernel(tc, x, offs, out):
     nc = tc.nc
-    x_blocks = x.rearrange("(b p) s -> b p s", p=P)
-    out_blocks = out.rearrange("(b p) t -> b p t", p=P)
+    x_pairs = x.rearrange("(g p j) s -> g j p s", p=P, j=PAIR)
+    out_pairs = out.rearrange("(g p j) t -> g p (j t)", p=P, j=PAIR)
 
     with (
         tc.tile_pool(name="held", bufs=1) as held,
@@ -36,7 +37,7 @@ def tile_ht_kernel(tc, x, offs, out):
             votes = []
             for lane in range(LANES):
                 pixels.append(blocks.tile([P, PIXELS], F32, name="pixels"))
-                nc.sync.dma_start(pixels[lane][:], x_blocks[first + lane])
+                nc.sync.dma_start(pixels[lane][:], x_pairs[(first + lane) // PAIR][(first + lane) % PAIR])
                 if first + lane == 0:
                     nc.sync.dma_start(offsets[:], offs)
                 votes.append(blocks.tile([P, PIXELS], F32, name="votes"))
@@ -50,12 +51,17 @@ def tile_ht_kernel(tc, x, offs, out):
                 sums.append(ring.tile([P, BINS], F32, name="sums"))
                 nc.scalar.activation(sums[lane][:], unrectified[:], RELU, scale=1.0 / WIDTH)
 
-            for k in range(1, VOTERS):
+            for k in range(1, VOTERS - 1):
                 for lane in range(LANES):
                     earlier = sums[lane]
                     sums[lane] = ring.tile([P, BINS], F32, name="sums")
                     picked = votes[lane][:].indirect(offsets[:, k * PIECE : (k + 1) * PIECE])
                     nc.vector.tensor_tensor(sums[lane][:], picked, earlier[:], ADD)
 
-            for lane in range(LANES):
-                nc.scalar.dma_start(out_blocks[first + lane], sums[lane][:])
+            for pair in range(LANES // PAIR):
+                done = blocks.tile([P, PAIR * BINS], F32, name="done")
+                for j in range(PAIR):
+                    lane = pair * PAIR + j
+                    picked = votes[lane][:].indirect(offsets[:, (VOTERS - 1) * PIECE : VOTERS * PIECE])
+                    nc.vector.tensor_tensor(done[:, j * BINS : (j + 1) * BINS], picked, sums[lane][:], ADD)
+                nc.scalar.dma_start(out_pairs[first // PAIR + pair], done[:])

@@ -60,8 +60,13 @@ def tile_ht_kernel(tc, x, offs, out):
 
             for pair in range(LANES // PAIR):
                 done = blocks.tile([P, PAIR * BINS], F32, name="done")
+                singly = first + (pair + 1) * PAIR == BLOCKS
                 for j in range(PAIR):
                     lane = pair * PAIR + j
+                    half = slice(j * BINS, (j + 1) * BINS)
                     picked = votes[lane][:].indirect(offsets[:, (VOTERS - 1) * PIECE : VOTERS * PIECE])
-                    nc.vector.tensor_tensor(done[:, j * BINS : (j + 1) * BINS], picked, sums[lane][:], ADD)
-                nc.scalar.dma_start(out_pairs[first // PAIR + pair], done[:])
+                    nc.vector.tensor_tensor(done[:, half], picked, sums[lane][:], ADD)
+                    if singly:
+                        nc.scalar.dma_start(out_pairs[first // PAIR + pair][:, half], done[:, half])
+                if not singly:
+                    nc.scalar.dma_start(out_pairs[first // PAIR + pair], done[:])

@@ -13,14 +13,15 @@ VOTERS = 8
 WIDTH = 16
 BLOCKS = PLANES // P
 PIECE = BINS // 16
-PAIR = 2
 LANES = 8
+STORES = (4, 2, 1, 1)
 
 
 def tile_ht_kernel(tc, x, offs, out):
     nc = tc.nc
-    x_pairs = x.rearrange("(g p j) s -> g j p s", p=P, j=PAIR)
-    out_pairs = out.rearrange("(g p j) t -> g p (j t)", p=P, j=PAIR)
+    x_blocks = x.rearrange("(p b) s -> b p s", b=BLOCKS)
+    out_rows = out.rearrange("(p b) t -> p (b t)", b=BLOCKS)
+    store_ends = [sum(STORES[: n + 1]) for n in range(len(STORES))]
 
     with (
         tc.tile_pool(name="held", bufs=1) as held,
@@ -32,12 +33,14 @@ def tile_ht_kernel(tc, x, offs, out):
         zeros = held.tile([P, BINS], F32, name="zeros")
         nc.vector.memset(zeros[:], 0.0)
 
+        done = held.tile([P, BLOCKS * BINS], F32, name="done")
+
         for first in range(0, BLOCKS, LANES):
             pixels = []
             votes = []
             for lane in range(LANES):
                 pixels.append(blocks.tile([P, PIXELS], F32, name="pixels"))
-                nc.sync.dma_start(pixels[lane][:], x_pairs[(first + lane) // PAIR][(first + lane) % PAIR])
+                nc.sync.dma_start(pixels[lane][:], x_blocks[first + lane])
                 if first + lane == 0:
                     nc.sync.dma_start(offsets[:], offs)
                 votes.append(blocks.tile([P, PIXELS], F32, name="votes"))
@@ -58,15 +61,11 @@ def tile_ht_kernel(tc, x, offs, out):
                     picked = votes[lane][:].indirect(offsets[:, k * PIECE : (k + 1) * PIECE])
                     nc.vector.tensor_tensor(sums[lane][:], picked, earlier[:], ADD)
 
-            for pair in range(LANES // PAIR):
-                done = blocks.tile([P, PAIR * BINS], F32, name="done")
-                singly = first + (pair + 1) * PAIR == BLOCKS
-                for j in range(PAIR):
-                    lane = pair * PAIR + j
-                    half = slice(j * BINS, (j + 1) * BINS)
-                    picked = votes[lane][:].indirect(offsets[:, (VOTERS - 1) * PIECE : VOTERS * PIECE])
-                    nc.vector.tensor_tensor(done[:, half], picked, sums[lane][:], ADD)
-                    if singly:
-                        nc.scalar.dma_start(out_pairs[first // PAIR + pair][:, half], done[:, half])
-                if not singly:
-                    nc.scalar.dma_start(out_pairs[first // PAIR + pair], done[:])
+            for lane in range(LANES):
+                block = first + lane
+                picked = votes[lane][:].indirect(offsets[:, (VOTERS - 1) * PIECE : VOTERS * PIECE])
+                nc.vector.tensor_tensor(done[:, block * BINS : (block + 1) * BINS], picked, sums[lane][:], ADD)
+                if block + 1 in store_ends:
+                    taken = STORES[store_ends.index(block + 1)]
+                    columns = slice((block + 1 - taken) * BINS, (block + 1) * BINS)
+                    nc.scalar.dma_start(out_rows[:, columns], done[:, columns])

@@ -13,7 +13,7 @@ VOTERS = 8
 WIDTH = 16
 BLOCKS = PLANES // P
 PIECE = BINS // 16
-LANES = 8
+LANES = 4
 STORES = (4, 2, 1, 1)
 
 

import concourse.mybir as mybir

F32 = mybir.dt.float32
U16 = mybir.dt.uint16
ADD = mybir.AluOpType.add
RELU = mybir.ActivationFunctionType.Relu

P = 128
PLANES = 1024
PIXELS = 256
BINS = 256
VOTERS = 8
WIDTH = 16
BLOCKS = PLANES // P
PIECE = BINS // 16
LANES = 4
STORES = (4, 2, 1, 1)


def tile_ht_kernel(tc, x, offs, out):
    nc = tc.nc
    x_blocks = x.rearrange("(p b) s -> b p s", b=BLOCKS)
    out_rows = out.rearrange("(p b) t -> p (b t)", b=BLOCKS)
    store_ends = [sum(STORES[: n + 1]) for n in range(len(STORES))]

    with (
        tc.tile_pool(name="held", bufs=1) as held,
        tc.tile_pool(name="blocks", bufs=BLOCKS) as blocks,
        tc.tile_pool(name="ring", bufs=LANES * VOTERS) as ring,
    ):
        offsets = held.tile([P, VOTERS * PIECE], U16, name="offsets")

        zeros = held.tile([P, BINS], F32, name="zeros")
        nc.vector.memset(zeros[:], 0.0)

        done = held.tile([P, BLOCKS * BINS], F32, name="done")

        for first in range(0, BLOCKS, LANES):
            pixels = []
            votes = []
            for lane in range(LANES):
                pixels.append(blocks.tile([P, PIXELS], F32, name="pixels"))
                nc.sync.dma_start(pixels[lane][:], x_blocks[first + lane])
                if first + lane == 0:
                    nc.sync.dma_start(offsets[:], offs)
                votes.append(blocks.tile([P, PIXELS], F32, name="votes"))
                nc.scalar.activation(votes[lane][:], pixels[lane][:], RELU, scale=1.0 / WIDTH)

            sums = []
            for lane in range(LANES):
                unrectified = ring.tile([P, BINS], F32, name="unrectified")
                picked = pixels[lane][:].indirect(offsets[:, 0:PIECE])
                nc.vector.tensor_tensor(unrectified[:], picked, zeros[:], ADD)
                sums.append(ring.tile([P, BINS], F32, name="sums"))
                nc.scalar.activation(sums[lane][:], unrectified[:], RELU, scale=1.0 / WIDTH)

            for k in range(1, VOTERS - 1):
                for lane in range(LANES):
                    earlier = sums[lane]
                    sums[lane] = ring.tile([P, BINS], F32, name="sums")
                    picked = votes[lane][:].indirect(offsets[:, k * PIECE : (k + 1) * PIECE])
                    nc.vector.tensor_tensor(sums[lane][:], picked, earlier[:], ADD)

            for lane in range(LANES):
                block = first + lane
                picked = votes[lane][:].indirect(offsets[:, (VOTERS - 1) * PIECE : VOTERS * PIECE])
                nc.vector.tensor_tensor(done[:, block * BINS : (block + 1) * BINS], picked, sums[lane][:], ADD)
                if block + 1 in store_ends:
                    taken = STORES[store_ends.index(block + 1)]
                    columns = slice((block + 1 - taken) * BINS, (block + 1) * BINS)
                    nc.scalar.dma_start(out_rows[:, columns], done[:, columns])
